import numpy as np
import ml_dtypes


def mxq(x, axis, fmt="e4m3"):
    dtype, down = {"e4m3": (ml_dtypes.float8_e4m3fn, 7), "e5m2": (ml_dtypes.float8_e5m2, 14)}[fmt]
    v = np.moveaxis(np.asarray(x, np.float32).astype(ml_dtypes.bfloat16).astype(np.float64), axis, -1)
    blocks = v.reshape(v.shape[:-1] + (-1, 32))
    amax = np.abs(blocks).max(-1, keepdims=True)
    byte = np.maximum(np.where(amax > 0, np.frexp(amax)[1] - 1 + 127, 0) - down, 1)
    scale = np.exp2(byte - 127.0)
    codes = (blocks / scale).astype(np.float32).astype(dtype).astype(np.float64)
    return np.moveaxis((codes * scale).reshape(v.shape), -1, axis)


WIDE = False


def mx_kscale(k):
    if not WIDE:
        return np.ones(k)
    levels = np.array([10, -10, 5, -5, 0])
    a = np.random.permutation(np.resize(levels, k // 512 * 4)).reshape(k // 512, 4)
    idx = np.arange(k)
    return np.exp2(a[idx // 512, idx % 128 // 32])


BF16 = ml_dtypes.bfloat16


def bf(x):
    return np.asarray(x, np.float32).astype(BF16)


def f64(x):
    return np.asarray(x).astype(np.float64)


B, S, D, H, NOPE, ROPE, VD, KV_RANK, Q_RANK = 2, 2048, 1024, 2, 64, 128, 64, 512, 1536
EPS = 1e-6
THETA = 10000.0
LAT = 0.005
PE = 0.1
HALF = ROPE // 2


def rmsnorm(v, g):
    return v * (1.0 / np.sqrt(np.mean(v * v, axis=-1, keepdims=True) + EPS)) * g


def rope(v):
    inv = 1.0 / THETA ** (np.arange(HALF) / HALF)
    ang = np.arange(S)[:, None] * inv[None, :]
    cos = np.cos(ang)[None, :, None, :]
    sin = np.sin(ang)[None, :, None, :]
    v1, v2 = v[..., :HALF], v[..., HALF:]
    return np.concatenate([v1 * cos - v2 * sin, v2 * cos + v1 * sin], axis=-1)


def setup_inputs():
    s, t = mx_kscale(D), mx_kscale(KV_RANK)
    col = np.concatenate([np.full(KV_RANK, LAT), np.full(ROPE, PE)]) / np.sqrt(D)
    return {"x": bf(np.random.standard_normal((B, S, D)) * s),
            "w_dkv": bf(np.random.standard_normal((D, KV_RANK + ROPE)) * col / s[:, None]),
            "kv_a_norm": bf((1.0 + 0.1 * np.random.standard_normal(KV_RANK)) * t),
            "w_ukv": bf(np.random.standard_normal((KV_RANK, H * (NOPE + VD))) / np.sqrt(KV_RANK) / t[:, None])}


def reference(x, w_dkv, kv_a_norm, w_ukv):
    xq = mxq(f64(x), 2, "e4m3")
    wd = f64(w_dkv)
    c_kv = xq @ mxq(wd[:, :KV_RANK], 0, "e4m3")
    k_pe = xq @ mxq(wd[:, KV_RANK:], 0, "e4m3")
    h = rmsnorm(c_kv, f64(kv_a_norm))
    kv = (mxq(h, 2, "e4m3") @ mxq(f64(w_ukv), 0, "e4m3")).reshape(B, S, H, NOPE + VD)
    k_nope, v = kv[..., :NOPE], kv[..., NOPE:]
    k_pe = rope(k_pe[:, :, None, :])
    kf = np.concatenate([k_nope, np.broadcast_to(k_pe, (B, S, H, ROPE))], axis=-1)
    return kf, v

@@ -1,0 +1,293 @@
+import math
+from contextlib import ExitStack
+
+import concourse.mybir as mybir
+from concourse.masks import make_identity
+
+F32 = mybir.dt.float32
+BF16 = mybir.dt.bfloat16
+I32 = mybir.dt.int32
+U32 = mybir.dt.uint32
+U8 = mybir.dt.uint8
+FP8X4 = mybir.dt.float8_e4m3fn_x4
+ALU = mybir.AluOpType
+ACT = mybir.ActivationFunctionType
+
+P = 128
+PACK = 4
+K_PASS = P * PACK
+
+TOKENS = 2 * 2048
+SEQ = 2048
+D_MODEL = 1024
+LATENT = 512
+ROPE = 128
+HALF = ROPE // 2
+HEADS = 2
+NOPE = 64
+V_DIM = 64
+KV_OUT = HEADS * (NOPE + V_DIM)
+KF_ROW = HEADS * (NOPE + ROPE)
+V_ROW = HEADS * V_DIM
+EPS = 1e-6
+THETA = 10000.0
+
+X_PASSES = D_MODEL // K_PASS
+TILES = 2
+ROUND = TILES * P
+ROUNDS = TOKENS // ROUND
+SEQ_ROUNDS = SEQ // ROUND
+
+ROUND_MAGIC = 12582912.0
+
+FLOPS = 2 * TOKENS * D_MODEL * (LATENT + ROPE) + 2 * TOKENS * LATENT * KV_OUT
+
+
+def tile_multiheadlatentattention_pb_t_kernel(tc, x, w_dkv, kv_a_norm, w_ukv, out_0, out_1):
+    nc = tc.nc
+    x_rows = x.flatten_outer_dims()
+    kf_rows = out_0.rearrange("b s h f -> (b s) (h f)")
+    v_rows = out_1.rearrange("b s h f -> (b s) (h f)")
+
+    with ExitStack() as ctx:
+        keep = ctx.enter_context(tc.tile_pool(name="keep", bufs=1))
+        x_pool = ctx.enter_context(tc.tile_pool(name="x_pool", bufs=ROUNDS))
+        work = ctx.enter_context(tc.tile_pool(name="work", bufs=4))
+        psum_x = ctx.enter_context(tc.psum_pool(name="psum_x", bufs=2))
+        psum_c = ctx.enter_context(tc.psum_pool(name="psum_c", bufs=3))
+        psum_one = ctx.enter_context(tc.psum_pool(name="psum_one", bufs=1))
+
+        wd_raw = keep.tile([P, X_PASSES, PACK, LATENT + ROPE], BF16)
+        for g in range(X_PASSES):
+            nc.sync.dma_start(
+                out=wd_raw[:, g].rearrange("p (u e) c -> p u (e c)", u=2),
+                in_=w_dkv[g * K_PASS : (g + 1) * K_PASS, :].rearrange("(u p e) c -> p u (e c)", u=2, e=2),
+            )
+        x_sb = {}
+        for i in range(ROUNDS):
+            x_sb[i] = x_pool.tile([P, TILES * D_MODEL], BF16, name="x_sb")
+            nc.sync.dma_start(
+                out=x_sb[i][:],
+                in_=x_rows[i * ROUND : (i + 1) * ROUND, :].rearrange("(p n) d -> p (n d)", n=TILES),
+            )
+        wu_raw = keep.tile([P, PACK, KV_OUT], BF16)
+        nc.scalar.dma_start(out=wu_raw[:], in_=w_ukv.rearrange("(t p) n -> p t n", p=P))
+        gain = keep.tile([P, LATENT], BF16)
+        nc.scalar.dma_start(out=gain[:], in_=kv_a_norm.partition_broadcast(P))
+
+        ident_f32 = keep.tile([P, P], F32)
+        make_identity(nc, ident_f32[:])
+        ident_bf16 = keep.tile([P, P], BF16)
+        make_identity(nc, ident_bf16[:])
+
+        n_pos = SEQ // P
+        pos_int = keep.tile([P, n_pos], I32)
+        nc.gpsimd.iota(pos_int[:], pattern=[[ROUND, SEQ_ROUNDS], [1, TILES]], base=0, channel_multiplier=TILES)
+        pos = keep.tile([P, n_pos], F32)
+        nc.vector.tensor_copy(out=pos[:], in_=pos_int[:])
+        one = keep.tile([P, 1], F32)
+        nc.vector.memset(one[:], 1.0)
+        freq = keep.tile([P, HALF], F32)
+        nc.vector.tensor_scalar_mul(out=freq[:, 0:1], in0=one[:], scalar1=1.0 / (2.0 * math.pi))
+        filled = 1
+        while filled < HALF:
+            nc.vector.tensor_scalar_mul(
+                out=freq[:, filled : 2 * filled], in0=freq[:, 0:filled], scalar1=THETA ** (-filled / HALF)
+            )
+            filled *= 2
+        table_shape = [P, n_pos, HALF]
+        turns = keep.tile(table_shape, F32)
+        nc.vector.tensor_tensor(
+            out=turns[:],
+            in0=pos[:].unsqueeze(2).to_broadcast(table_shape),
+            in1=freq[:].unsqueeze(1).to_broadcast(table_shape),
+            op=ALU.mult,
+        )
+        whole = keep.tile(table_shape, F32)
+        nc.vector.tensor_scalar(
+            out=whole[:], in0=turns[:], scalar1=ROUND_MAGIC, scalar2=ROUND_MAGIC, op0=ALU.add, op1=ALU.subtract
+        )
+        frac = keep.tile(table_shape, F32)
+        nc.vector.tensor_tensor(out=frac[:], in0=turns[:], in1=whole[:], op=ALU.subtract)
+        neg_abs = keep.tile(table_shape, F32)
+        nc.vector.scalar_tensor_tensor(
+            out=neg_abs[:], in0=frac[:], scalar=-1.0, in1=frac[:], op0=ALU.mult, op1=ALU.min
+        )
+        quarter_turn = keep.tile([P, 1], F32)
+        nc.vector.tensor_scalar_mul(out=quarter_turn[:], in0=one[:], scalar1=math.pi / 2.0)
+        sin_t = keep.tile(table_shape, F32)
+        nc.scalar.activation(out=sin_t[:], in_=frac[:], func=ACT.Sin, scale=2.0 * math.pi)
+        cos_t = keep.tile(table_shape, F32)
+        nc.scalar.activation(
+            out=cos_t[:], in_=neg_abs[:], func=ACT.Sin, bias=quarter_turn[:], scale=2.0 * math.pi
+        )
+        eps = keep.tile([P, 1], F32)
+        nc.vector.tensor_scalar_mul(out=eps[:], in0=one[:], scalar1=EPS)
+
+        wd_grouped = keep.tile([P, X_PASSES, LATENT + ROPE, PACK], BF16, align_bytes=64)
+        wd_codes = keep.tile([P, X_PASSES, LATENT + ROPE], U32, align_bytes=64)
+        wd_scales = keep.tile([P, X_PASSES, LATENT + ROPE], U8, align_bytes=64)
+        for g in range(X_PASSES):
+            nc.vector.tensor_copy(out=wd_grouped[:, g], in_=wd_raw[:, g].rearrange("p t c -> p c t"))
+        for g in range(X_PASSES):
+            for cols in (slice(0, LATENT), slice(LATENT, LATENT + ROPE)):
+                nc.vector.quantize_mx(
+                    out=wd_codes[:, g, cols].bitcast(FP8X4),
+                    scales=wd_scales[:, g, cols],
+                    in_=wd_grouped[:, g, cols, :].rearrange("p c t -> p (c t)"),
+                )
+        wu_grouped = keep.tile([P, KV_OUT, PACK], BF16, align_bytes=64)
+        wu_codes = keep.tile([P, KV_OUT], U32, align_bytes=64)
+        wu_scales = keep.tile([P, KV_OUT], U8, align_bytes=64)
+        nc.vector.tensor_copy(out=wu_grouped[:], in_=wu_raw[:].rearrange("p t n -> p n t"))
+        nc.vector.quantize_mx(
+            out=wu_codes[:].bitcast(FP8X4),
+            scales=wu_scales[:],
+            in_=wu_grouped[:].rearrange("p n t -> p (n t)"),
+        )
+
+        x_codes, x_scales = {}, {}
+        latent_ps, key_ps, sum_sq, rms = {}, {}, {}, {}
+        h_sb, h_codes, h_scales = {}, {}, {}
+        kf_sb = {}
+
+        def transpose_x(i):
+            words = x_sb[i][:].bitcast(F32)
+            n_words = D_MODEL // 2
+            grouped = work.tile([P, TILES * n_words], F32, name="x_grouped", align_bytes=64)
+            for n in range(TILES):
+                xt_ps = psum_x.tile([P, 2 * X_PASSES, P], F32, name="xt_ps")
+                for a in range(2 * X_PASSES):
+                    first = n * n_words + a * P
+                    nc.tensor.transpose(xt_ps[:, a, :], words[:, first : first + P], ident_f32[:])
+                copy = nc.scalar.copy if n == 0 else nc.vector.tensor_copy
+                copy(
+                    out=grouped[:, n * n_words : (n + 1) * n_words].rearrange(
+                        "p (g r u) -> p g r u", g=X_PASSES, u=2
+                    ),
+                    in_=xt_ps[:].rearrange("p (g u) r -> p g r u", u=2),
+                )
+            x_codes[i] = work.tile([P, TILES * X_PASSES * P], U32, name="x_codes", align_bytes=64)
+            x_scales[i] = work.tile([P, TILES * X_PASSES * P], U8, name="x_scales", align_bytes=64)
+            nc.vector.quantize_mx(
+                out=x_codes[i][:].bitcast(FP8X4), scales=x_scales[i][:], in_=grouped[:].bitcast(BF16)
+            )
+
+        def down_project(i):
+            key_ps[i] = psum_one.tile([P, TILES, ROPE], F32, name="key_ps")
+            sum_sq[i] = work.tile([P, TILES], F32, name="sum_sq")
+            for n in range(TILES):
+                latent_ps[i, n] = psum_c.tile([P, LATENT], F32, name="latent_ps")
+                for out, cols in (
+                    (latent_ps[i, n][:], slice(0, LATENT)),
+                    (key_ps[i][:, n, :], slice(LATENT, LATENT + ROPE)),
+                ):
+                    for g in range(X_PASSES):
+                        tokens = slice((n * X_PASSES + g) * P, (n * X_PASSES + g + 1) * P)
+                        nc.tensor.matmul_mx(
+                            out=out,
+                            lhsT=x_codes[i][:, tokens].bitcast(FP8X4),
+                            lhsT_scale=x_scales[i][:, tokens],
+                            rhs=wd_codes[:, g, cols].bitcast(FP8X4),
+                            rhs_scale=wd_scales[:, g, cols],
+                            start=(g == 0),
+                            stop=(g == X_PASSES - 1),
+                        )
+                squares = work.tile([P, LATENT], BF16, name="squares")
+                nc.scalar.activation(
+                    out=squares[:], in_=latent_ps[i, n][:], func=ACT.Square, accum_out=sum_sq[i][:, n : n + 1]
+                )
+            rms[i] = work.tile([P, TILES], F32, name="rms")
+            nc.scalar.activation(out=rms[i][:], in_=sum_sq[i][:], func=ACT.Sqrt, bias=eps[:], scale=1.0 / LATENT)
+
+        def norm_and_rotate(i):
+            first = (i % SEQ_ROUNDS) * TILES
+            halves = [P, TILES, 2, HALF]
+            key = key_ps[i][:].rearrange("p n (a f) -> p n a f", a=2)
+            key_cos = work.tile(halves, F32, name="key_cos")
+            nc.vector.tensor_tensor(
+                out=key_cos[:], in0=key, in1=cos_t[:, first : first + TILES, :].unsqueeze(2).to_broadcast(halves),
+                op=ALU.mult,
+            )
+            key_sin = work.tile(halves, F32, name="key_sin")
+            nc.vector.tensor_tensor(
+                out=key_sin[:], in0=key, in1=sin_t[:, first : first + TILES, :].unsqueeze(2).to_broadcast(halves),
+                op=ALU.mult,
+            )
+            inv_rms = work.tile([P, TILES], F32, name="inv_rms")
+            nc.vector.reciprocal(out=inv_rms[:], in_=rms[i][:])
+            h_sb[i] = work.tile([P, TILES * LATENT], BF16, name="h_sb")
+            for n in range(TILES):
+                nc.vector.scalar_tensor_tensor(
+                    out=h_sb[i][:, n * LATENT : (n + 1) * LATENT],
+                    in0=latent_ps[i, n][:],
+                    scalar=inv_rms[:, n : n + 1],
+                    in1=gain[:],
+                    op0=ALU.mult,
+                    op1=ALU.mult,
+                )
+            kf_sb[i] = work.tile([P, TILES * KF_ROW], F32, name="kf_sb", bufs=6)
+            kf = kf_sb[i][:].rearrange("p (n h f) -> p n h f", n=TILES, h=HEADS)
+            per_head = [P, TILES, HEADS, HALF]
+            nc.vector.tensor_tensor(
+                out=kf[:, :, :, NOPE : NOPE + HALF],
+                in0=key_cos[:, :, 0, :].unsqueeze(2).to_broadcast(per_head),
+                in1=key_sin[:, :, 1, :].unsqueeze(2).to_broadcast(per_head),
+                op=ALU.subtract,
+            )
+            nc.vector.tensor_tensor(
+                out=kf[:, :, :, NOPE + HALF : NOPE + ROPE],
+                in0=key_cos[:, :, 1, :].unsqueeze(2).to_broadcast(per_head),
+                in1=key_sin[:, :, 0, :].unsqueeze(2).to_broadcast(per_head),
+                op=ALU.add,
+            )
+
+        def transpose_h(i):
+            ht_ps = psum_one.tile([P, TILES, PACK, P], BF16, name="ht_ps")
+            for n in range(TILES):
+                for t in range(PACK):
+                    first = n * LATENT + t * P
+                    nc.tensor.transpose(ht_ps[:, n, t, :], h_sb[i][:, first : first + P], ident_bf16[:])
+            grouped = work.tile([P, TILES * P * PACK], BF16, name="h_grouped", align_bytes=64)
+            nc.scalar.copy(
+                out=grouped[:].rearrange("p (n r t) -> p n r t", n=TILES, t=PACK),
+                in_=ht_ps[:].rearrange("p n t r -> p n r t"),
+            )
+            h_codes[i] = work.tile([P, TILES * P], U32, name="h_codes", align_bytes=64)
+            h_scales[i] = work.tile([P, TILES * P], U8, name="h_scales", align_bytes=64)
+            nc.vector.quantize_mx(out=h_codes[i][:].bitcast(FP8X4), scales=h_scales[i][:], in_=grouped[:])
+
+        def up_project_and_store(i):
+            kv_ps = psum_one.tile([P, TILES, KV_OUT], F32, name="kv_ps")
+            for n in range(TILES):
+                tokens = slice(n * P, (n + 1) * P)
+                nc.tensor.matmul_mx(
+                    out=kv_ps[:, n, :],
+                    lhsT=h_codes[i][:, tokens].bitcast(FP8X4),
+                    lhsT_scale=h_scales[i][:, tokens],
+                    rhs=wu_codes[:].bitcast(FP8X4),
+                    rhs_scale=wu_scales[:],
+                    start=True,
+                    stop=True,
+                )
+            kv = kv_ps[:].rearrange("p n (h f) -> p n h f", h=HEADS)
+            kf = kf_sb[i][:].rearrange("p (n h f) -> p n h f", n=TILES, h=HEADS)
+            nc.scalar.copy(out=kf[:, :, :, 0:NOPE], in_=kv[:, :, :, 0:NOPE])
+            v_sb = work.tile([P, TILES * V_ROW], F32, name="v_sb")
+            nc.scalar.copy(
+                out=v_sb[:].rearrange("p (n h f) -> p n h f", n=TILES, h=HEADS), in_=kv[:, :, :, NOPE : NOPE + V_DIM]
+            )
+            rows = slice(i * ROUND, (i + 1) * ROUND)
+            nc.sync.dma_start(out=kf_rows[rows, :].rearrange("(p n) f -> p (n f)", n=TILES), in_=kf_sb[i][:])
+            nc.sync.dma_start(out=v_rows[rows, :].rearrange("(p n) f -> p (n f)", n=TILES), in_=v_sb[:])
+
+        def run(stage, i):
+            if 0 <= i < ROUNDS:
+                stage(i)
+
+        for step in range(ROUNDS + 4):
+            run(norm_and_rotate, step - 2)
+            run(transpose_x, step)
+            run(transpose_h, step - 3)
+            run(down_project, step - 1)
+            run(up_project_and_store, step - 4)

@@ -56,6 +56,7 @@ def tile_multiheadlatentattention_pb_t_kernel(tc, x, w_dkv, kv_a_norm, w_ukv, ou
         psum_x = ctx.enter_context(tc.psum_pool(name="psum_x", bufs=2))
         psum_c = ctx.enter_context(tc.psum_pool(name="psum_c", bufs=3))
         psum_one = ctx.enter_context(tc.psum_pool(name="psum_one", bufs=1))
+        ctx.enter_context(tc.manual_schedule())
 
         wd_raw = keep.tile([P, X_PASSES, PACK, LATENT + ROPE], BF16)
         for g in range(X_PASSES):

@@ -72,14 +72,15 @@ def tile_multiheadlatentattention_pb_t_kernel(tc, x, w_dkv, kv_a_norm, w_ukv, ou
                 in_=x_rows[i * ROUND : (i + 1) * ROUND, :].rearrange("(p n) d -> p (n d)", n=TILES),
             )
         wu_raw = keep.tile([P, PACK, KV_OUT], BF16)
-        nc.scalar.dma_start(out=wu_raw[:], in_=w_ukv.rearrange("(t p) n -> p t n", p=P))
+        nc.scalar.dma_start(
+            out=wu_raw[:].rearrange("p (u e) n -> p u (e n)", u=2),
+            in_=w_ukv.rearrange("(u p e) n -> p u (e n)", u=2, e=2),
+        )
         gain = keep.tile([P, LATENT], BF16)
         nc.scalar.dma_start(out=gain[:], in_=kv_a_norm.partition_broadcast(P))
 
         ident_f32 = keep.tile([P, P], F32)
         make_identity(nc, ident_f32[:])
-        ident_bf16 = keep.tile([P, P], BF16)
-        make_identity(nc, ident_bf16[:])
 
         n_pos = SEQ // P
         pos_int = keep.tile([P, n_pos], I32)
@@ -110,17 +111,15 @@ def tile_multiheadlatentattention_pb_t_kernel(tc, x, w_dkv, kv_a_norm, w_ukv, ou
         )
         frac = keep.tile(table_shape, F32)
         nc.vector.tensor_tensor(out=frac[:], in0=turns[:], in1=whole[:], op=ALU.subtract)
-        neg_abs = keep.tile(table_shape, F32)
-        nc.vector.scalar_tensor_tensor(
-            out=neg_abs[:], in0=frac[:], scalar=-1.0, in1=frac[:], op0=ALU.mult, op1=ALU.min
-        )
         quarter_turn = keep.tile([P, 1], F32)
         nc.vector.tensor_scalar_mul(out=quarter_turn[:], in0=one[:], scalar1=math.pi / 2.0)
         sin_t = keep.tile(table_shape, F32)
         nc.scalar.activation(out=sin_t[:], in_=frac[:], func=ACT.Sin, scale=2.0 * math.pi)
+        abs_frac = keep.tile(table_shape, F32)
+        nc.scalar.activation(out=abs_frac[:], in_=frac[:], func=ACT.Abs)
         cos_t = keep.tile(table_shape, F32)
         nc.scalar.activation(
-            out=cos_t[:], in_=neg_abs[:], func=ACT.Sin, bias=quarter_turn[:], scale=2.0 * math.pi
+            out=cos_t[:], in_=abs_frac[:], func=ACT.Sin, bias=quarter_turn[:], scale=-2.0 * math.pi
         )
         eps = keep.tile([P, 1], F32)
         nc.vector.tensor_scalar_mul(out=eps[:], in0=one[:], scalar1=EPS)
@@ -230,13 +229,13 @@ def tile_multiheadlatentattention_pb_t_kernel(tc, x, w_dkv, kv_a_norm, w_ukv, ou
             kf_sb[i] = work.tile([P, TILES * KF_ROW], F32, name="kf_sb", bufs=6)
             kf = kf_sb[i][:].rearrange("p (n h f) -> p n h f", n=TILES, h=HEADS)
             per_head = [P, TILES, HEADS, HALF]
-            nc.vector.tensor_tensor(
+            nc.gpsimd.tensor_tensor(
                 out=kf[:, :, :, NOPE : NOPE + HALF],
                 in0=key_cos[:, :, 0, :].unsqueeze(2).to_broadcast(per_head),
                 in1=key_sin[:, :, 1, :].unsqueeze(2).to_broadcast(per_head),
                 op=ALU.subtract,
             )
-            nc.vector.tensor_tensor(
+            nc.gpsimd.tensor_tensor(
                 out=kf[:, :, :, NOPE + HALF : NOPE + ROPE],
                 in0=key_cos[:, :, 1, :].unsqueeze(2).to_broadcast(per_head),
                 in1=key_sin[:, :, 0, :].unsqueeze(2).to_broadcast(per_head),
@@ -244,19 +243,23 @@ def tile_multiheadlatentattention_pb_t_kernel(tc, x, w_dkv, kv_a_norm, w_ukv, ou
             )
 
         def transpose_h(i):
-            ht_ps = psum_one.tile([P, TILES, PACK, P], BF16, name="ht_ps")
+            words = h_sb[i][:].bitcast(F32)
+            n_words = LATENT // 2
+            ht_ps = psum_one.tile([P, TILES, 2, P], F32, name="ht_ps")
             for n in range(TILES):
-                for t in range(PACK):
-                    first = n * LATENT + t * P
-                    nc.tensor.transpose(ht_ps[:, n, t, :], h_sb[i][:, first : first + P], ident_bf16[:])
-            grouped = work.tile([P, TILES * P * PACK], BF16, name="h_grouped", align_bytes=64)
+                for u in range(2):
+                    first = n * n_words + u * P
+                    nc.tensor.transpose(ht_ps[:, n, u, :], words[:, first : first + P], ident_f32[:])
+            grouped = work.tile([P, TILES * n_words], F32, name="h_grouped", align_bytes=64)
             nc.scalar.copy(
-                out=grouped[:].rearrange("p (n r t) -> p n r t", n=TILES, t=PACK),
-                in_=ht_ps[:].rearrange("p n t r -> p n r t"),
+                out=grouped[:].rearrange("p (n r u) -> p n r u", n=TILES, u=2),
+                in_=ht_ps[:].rearrange("p n u r -> p n r u"),
             )
             h_codes[i] = work.tile([P, TILES * P], U32, name="h_codes", align_bytes=64)
             h_scales[i] = work.tile([P, TILES * P], U8, name="h_scales", align_bytes=64)
-            nc.vector.quantize_mx(out=h_codes[i][:].bitcast(FP8X4), scales=h_scales[i][:], in_=grouped[:])
+            nc.vector.quantize_mx(
+                out=h_codes[i][:].bitcast(FP8X4), scales=h_scales[i][:], in_=grouped[:].bitcast(BF16)
+            )
 
         def up_project_and_store(i):
             kv_ps = psum_one.tile([P, TILES, KV_OUT], F32, name="kv_ps")

@@ -27,8 +27,6 @@ HEADS = 2
 NOPE = 64
 V_DIM = 64
 KV_OUT = HEADS * (NOPE + V_DIM)
-KF_ROW = HEADS * (NOPE + ROPE)
-V_ROW = HEADS * V_DIM
 EPS = 1e-6
 THETA = 10000.0
 
@@ -46,7 +44,7 @@ FLOPS = 2 * TOKENS * D_MODEL * (LATENT + ROPE) + 2 * TOKENS * LATENT * KV_OUT
 def tile_multiheadlatentattention_pb_t_kernel(tc, x, w_dkv, kv_a_norm, w_ukv, out_0, out_1):
     nc = tc.nc
     x_rows = x.flatten_outer_dims()
-    kf_rows = out_0.rearrange("b s h f -> (b s) (h f)")
+    kf_rows = out_0.rearrange("b s h f -> (b s) h f")
     v_rows = out_1.rearrange("b s h f -> (b s) (h f)")
 
     with ExitStack() as ctx:
@@ -79,14 +77,11 @@ def tile_multiheadlatentattention_pb_t_kernel(tc, x, w_dkv, kv_a_norm, w_ukv, ou
         gain = keep.tile([P, LATENT], BF16)
         nc.scalar.dma_start(out=gain[:], in_=kv_a_norm.partition_broadcast(P))
 
-        ident_f32 = keep.tile([P, P], F32)
-        make_identity(nc, ident_f32[:])
-
         n_pos = SEQ // P
         pos_int = keep.tile([P, n_pos], I32)
         nc.gpsimd.iota(pos_int[:], pattern=[[ROUND, SEQ_ROUNDS], [1, TILES]], base=0, channel_multiplier=TILES)
-        pos = keep.tile([P, n_pos], F32)
-        nc.vector.tensor_copy(out=pos[:], in_=pos_int[:])
+        identity = keep.tile([P, P], F32)
+        make_identity(nc, identity[:])
         one = keep.tile([P, 1], F32)
         nc.vector.memset(one[:], 1.0)
         freq = keep.tile([P, HALF], F32)
@@ -97,6 +92,8 @@ def tile_multiheadlatentattention_pb_t_kernel(tc, x, w_dkv, kv_a_norm, w_ukv, ou
                 out=freq[:, filled : 2 * filled], in0=freq[:, 0:filled], scalar1=THETA ** (-filled / HALF)
             )
             filled *= 2
+        pos = keep.tile([P, n_pos], F32)
+        nc.vector.tensor_copy(out=pos[:], in_=pos_int[:])
         table_shape = [P, n_pos, HALF]
         turns = keep.tile(table_shape, F32)
         nc.vector.tensor_tensor(
@@ -113,6 +110,12 @@ def tile_multiheadlatentattention_pb_t_kernel(tc, x, w_dkv, kv_a_norm, w_ukv, ou
         nc.vector.tensor_tensor(out=frac[:], in0=turns[:], in1=whole[:], op=ALU.subtract)
         quarter_turn = keep.tile([P, 1], F32)
         nc.vector.tensor_scalar_mul(out=quarter_turn[:], in0=one[:], scalar1=math.pi / 2.0)
+        eps = keep.tile([P, 1], F32)
+        nc.vector.tensor_scalar_mul(out=eps[:], in0=one[:], scalar1=EPS)
+
+        wu_grouped = keep.tile([P, KV_OUT, PACK], BF16, align_bytes=64)
+        nc.scalar.copy(out=wu_grouped[:], in_=wu_raw[:].rearrange("p t n -> p n t"))
+
         sin_t = keep.tile(table_shape, F32)
         nc.scalar.activation(out=sin_t[:], in_=frac[:], func=ACT.Sin, scale=2.0 * math.pi)
         abs_frac = keep.tile(table_shape, F32)
@@ -121,8 +124,6 @@ def tile_multiheadlatentattention_pb_t_kernel(tc, x, w_dkv, kv_a_norm, w_ukv, ou
         nc.scalar.activation(
             out=cos_t[:], in_=abs_frac[:], func=ACT.Sin, bias=quarter_turn[:], scale=-2.0 * math.pi
         )
-        eps = keep.tile([P, 1], F32)
-        nc.vector.tensor_scalar_mul(out=eps[:], in0=one[:], scalar1=EPS)
 
         wd_grouped = keep.tile([P, X_PASSES, LATENT + ROPE, PACK], BF16, align_bytes=64)
         wd_codes = keep.tile([P, X_PASSES, LATENT + ROPE], U32, align_bytes=64)
@@ -136,51 +137,50 @@ def tile_multiheadlatentattention_pb_t_kernel(tc, x, w_dkv, kv_a_norm, w_ukv, ou
                     scales=wd_scales[:, g, cols],
                     in_=wd_grouped[:, g, cols, :].rearrange("p c t -> p (c t)"),
                 )
-        wu_grouped = keep.tile([P, KV_OUT, PACK], BF16, align_bytes=64)
         wu_codes = keep.tile([P, KV_OUT], U32, align_bytes=64)
         wu_scales = keep.tile([P, KV_OUT], U8, align_bytes=64)
-        nc.vector.tensor_copy(out=wu_grouped[:], in_=wu_raw[:].rearrange("p t n -> p n t"))
         nc.vector.quantize_mx(
             out=wu_codes[:].bitcast(FP8X4),
             scales=wu_scales[:],
             in_=wu_grouped[:].rearrange("p n t -> p (n t)"),
         )
 
-        x_codes, x_scales = {}, {}
-        latent_ps, key_ps, sum_sq, rms = {}, {}, {}, {}
-        h_sb, h_codes, h_scales = {}, {}, {}
-        kf_sb = {}
+        x_grouped, x_codes, x_scales = {}, {}, {}
+        latent_ps, inv_rms, key_sb = {}, {}, {}
+        h_sb, h_grouped, h_codes, h_scales = {}, {}, {}, {}
 
         def transpose_x(i):
             words = x_sb[i][:].bitcast(F32)
             n_words = D_MODEL // 2
-            grouped = work.tile([P, TILES * n_words], F32, name="x_grouped", align_bytes=64)
+            x_grouped[i] = work.tile([P, TILES * n_words], F32, name="x_grouped", align_bytes=64)
             for n in range(TILES):
                 xt_ps = psum_x.tile([P, 2 * X_PASSES, P], F32, name="xt_ps")
                 for a in range(2 * X_PASSES):
                     first = n * n_words + a * P
-                    nc.tensor.transpose(xt_ps[:, a, :], words[:, first : first + P], ident_f32[:])
+                    nc.tensor.transpose(xt_ps[:, a, :], words[:, first : first + P], identity[:])
                 copy = nc.scalar.copy if n == 0 else nc.vector.tensor_copy
                 copy(
-                    out=grouped[:, n * n_words : (n + 1) * n_words].rearrange(
+                    out=x_grouped[i][:, n * n_words : (n + 1) * n_words].rearrange(
                         "p (g r u) -> p g r u", g=X_PASSES, u=2
                     ),
                     in_=xt_ps[:].rearrange("p (g u) r -> p g r u", u=2),
                 )
+
+        def quantise_x(i):
             x_codes[i] = work.tile([P, TILES * X_PASSES * P], U32, name="x_codes", align_bytes=64)
             x_scales[i] = work.tile([P, TILES * X_PASSES * P], U8, name="x_scales", align_bytes=64)
             nc.vector.quantize_mx(
-                out=x_codes[i][:].bitcast(FP8X4), scales=x_scales[i][:], in_=grouped[:].bitcast(BF16)
+                out=x_codes[i][:].bitcast(FP8X4), scales=x_scales[i][:], in_=x_grouped[i][:].bitcast(BF16)
             )
 
         def down_project(i):
-            key_ps[i] = psum_one.tile([P, TILES, ROPE], F32, name="key_ps")
-            sum_sq[i] = work.tile([P, TILES], F32, name="sum_sq")
+            key_ps = psum_one.tile([P, TILES, ROPE], F32, name="key_ps")
+            sum_sq = work.tile([P, TILES], F32, name="sum_sq")
             for n in range(TILES):
                 latent_ps[i, n] = psum_c.tile([P, LATENT], F32, name="latent_ps")
                 for out, cols in (
                     (latent_ps[i, n][:], slice(0, LATENT)),
-                    (key_ps[i][:, n, :], slice(LATENT, LATENT + ROPE)),
+                    (key_ps[:, n, :], slice(LATENT, LATENT + ROPE)),
                 ):
                     for g in range(X_PASSES):
                         tokens = slice((n * X_PASSES + g) * P, (n * X_PASSES + g + 1) * P)
@@ -195,52 +195,56 @@ def tile_multiheadlatentattention_pb_t_kernel(tc, x, w_dkv, kv_a_norm, w_ukv, ou
                         )
                 squares = work.tile([P, LATENT], BF16, name="squares")
                 nc.scalar.activation(
-                    out=squares[:], in_=latent_ps[i, n][:], func=ACT.Square, accum_out=sum_sq[i][:, n : n + 1]
+                    out=squares[:], in_=latent_ps[i, n][:], func=ACT.Square, accum_out=sum_sq[:, n : n + 1]
                 )
-            rms[i] = work.tile([P, TILES], F32, name="rms")
-            nc.scalar.activation(out=rms[i][:], in_=sum_sq[i][:], func=ACT.Sqrt, bias=eps[:], scale=1.0 / LATENT)
+            inv_rms[i] = work.tile([P, TILES], F32, name="inv_rms")
+            nc.scalar.activation(
+                out=inv_rms[i][:], in_=sum_sq[:], func=ACT.Abs_reciprocal_sqrt, bias=eps[:], scale=1.0 / LATENT
+            )
+            key_sb[i] = work.tile([P, TILES, 2, HALF], F32, name="key_sb")
+            nc.scalar.copy(out=key_sb[i][:].rearrange("p n a f -> p n (a f)"), in_=key_ps[:])
 
-        def norm_and_rotate(i):
+        def rotate_and_store(i):
             first = (i % SEQ_ROUNDS) * TILES
             halves = [P, TILES, 2, HALF]
-            key = key_ps[i][:].rearrange("p n (a f) -> p n a f", a=2)
             key_cos = work.tile(halves, F32, name="key_cos")
-            nc.vector.tensor_tensor(
-                out=key_cos[:], in0=key, in1=cos_t[:, first : first + TILES, :].unsqueeze(2).to_broadcast(halves),
+            nc.gpsimd.tensor_tensor(
+                out=key_cos[:],
+                in0=key_sb[i][:],
+                in1=cos_t[:, first : first + TILES, :].unsqueeze(2).to_broadcast(halves),
                 op=ALU.mult,
             )
             key_sin = work.tile(halves, F32, name="key_sin")
-            nc.vector.tensor_tensor(
-                out=key_sin[:], in0=key, in1=sin_t[:, first : first + TILES, :].unsqueeze(2).to_broadcast(halves),
+            nc.gpsimd.tensor_tensor(
+                out=key_sin[:],
+                in0=key_sb[i][:],
+                in1=sin_t[:, first : first + TILES, :].unsqueeze(2).to_broadcast(halves),
                 op=ALU.mult,
             )
-            inv_rms = work.tile([P, TILES], F32, name="inv_rms")
-            nc.vector.reciprocal(out=inv_rms[:], in_=rms[i][:])
+            rotated = work.tile(halves, F32, name="rotated")
+            nc.gpsimd.tensor_tensor(
+                out=rotated[:, :, 0, :], in0=key_cos[:, :, 0, :], in1=key_sin[:, :, 1, :], op=ALU.subtract
+            )
+            nc.gpsimd.tensor_tensor(
+                out=rotated[:, :, 1, :], in0=key_cos[:, :, 1, :], in1=key_sin[:, :, 0, :], op=ALU.add
+            )
+            kf = kf_rows[i * ROUND : (i + 1) * ROUND].rearrange("(p n) h f -> p n h f", n=TILES)
+            for head in range(HEADS):
+                nc.sync.dma_start(
+                    out=kf[:, :, head, NOPE : NOPE + ROPE], in_=rotated[:].rearrange("p n a f -> p n (a f)")
+                )
+
+        def normalise(i):
             h_sb[i] = work.tile([P, TILES * LATENT], BF16, name="h_sb")
             for n in range(TILES):
                 nc.vector.scalar_tensor_tensor(
                     out=h_sb[i][:, n * LATENT : (n + 1) * LATENT],
                     in0=latent_ps[i, n][:],
-                    scalar=inv_rms[:, n : n + 1],
+                    scalar=inv_rms[i][:, n : n + 1],
                     in1=gain[:],
                     op0=ALU.mult,
                     op1=ALU.mult,
                 )
-            kf_sb[i] = work.tile([P, TILES * KF_ROW], F32, name="kf_sb", bufs=6)
-            kf = kf_sb[i][:].rearrange("p (n h f) -> p n h f", n=TILES, h=HEADS)
-            per_head = [P, TILES, HEADS, HALF]
-            nc.gpsimd.tensor_tensor(
-                out=kf[:, :, :, NOPE : NOPE + HALF],
-                in0=key_cos[:, :, 0, :].unsqueeze(2).to_broadcast(per_head),
-                in1=key_sin[:, :, 1, :].unsqueeze(2).to_broadcast(per_head),
-                op=ALU.subtract,
-            )
-            nc.gpsimd.tensor_tensor(
-                out=kf[:, :, :, NOPE + HALF : NOPE + ROPE],
-                in0=key_cos[:, :, 1, :].unsqueeze(2).to_broadcast(per_head),
-                in1=key_sin[:, :, 0, :].unsqueeze(2).to_broadcast(per_head),
-                op=ALU.add,
-            )
 
         def transpose_h(i):
             words = h_sb[i][:].bitcast(F32)
@@ -249,16 +253,18 @@ def tile_multiheadlatentattention_pb_t_kernel(tc, x, w_dkv, kv_a_norm, w_ukv, ou
             for n in range(TILES):
                 for u in range(2):
                     first = n * n_words + u * P
-                    nc.tensor.transpose(ht_ps[:, n, u, :], words[:, first : first + P], ident_f32[:])
-            grouped = work.tile([P, TILES * n_words], F32, name="h_grouped", align_bytes=64)
-            nc.scalar.copy(
-                out=grouped[:].rearrange("p (n r u) -> p n r u", n=TILES, u=2),
+                    nc.tensor.transpose(ht_ps[:, n, u, :], words[:, first : first + P], identity[:])
+            h_grouped[i] = work.tile([P, TILES * n_words], F32, name="h_grouped", align_bytes=64)
+            nc.vector.tensor_copy(
+                out=h_grouped[i][:].rearrange("p (n r u) -> p n r u", n=TILES, u=2),
                 in_=ht_ps[:].rearrange("p n u r -> p n r u"),
             )
+
+        def quantise_h(i):
             h_codes[i] = work.tile([P, TILES * P], U32, name="h_codes", align_bytes=64)
             h_scales[i] = work.tile([P, TILES * P], U8, name="h_scales", align_bytes=64)
             nc.vector.quantize_mx(
-                out=h_codes[i][:].bitcast(FP8X4), scales=h_scales[i][:], in_=grouped[:].bitcast(BF16)
+                out=h_codes[i][:].bitcast(FP8X4), scales=h_scales[i][:], in_=h_grouped[i][:].bitcast(BF16)
             )
 
         def up_project_and_store(i):
@@ -275,23 +281,28 @@ def tile_multiheadlatentattention_pb_t_kernel(tc, x, w_dkv, kv_a_norm, w_ukv, ou
                     stop=True,
                 )
             kv = kv_ps[:].rearrange("p n (h f) -> p n h f", h=HEADS)
-            kf = kf_sb[i][:].rearrange("p (n h f) -> p n h f", n=TILES, h=HEADS)
-            nc.scalar.copy(out=kf[:, :, :, 0:NOPE], in_=kv[:, :, :, 0:NOPE])
-            v_sb = work.tile([P, TILES * V_ROW], F32, name="v_sb")
-            nc.scalar.copy(
-                out=v_sb[:].rearrange("p (n h f) -> p n h f", n=TILES, h=HEADS), in_=kv[:, :, :, NOPE : NOPE + V_DIM]
-            )
+            nope_sb = work.tile([P, TILES, HEADS, NOPE], F32, name="nope_sb")
+            nc.scalar.copy(out=nope_sb[:], in_=kv[:, :, :, 0:NOPE])
+            v_sb = work.tile([P, TILES, HEADS, V_DIM], F32, name="v_sb")
+            nc.scalar.copy(out=v_sb[:], in_=kv[:, :, :, NOPE : NOPE + V_DIM])
             rows = slice(i * ROUND, (i + 1) * ROUND)
-            nc.sync.dma_start(out=kf_rows[rows, :].rearrange("(p n) f -> p (n f)", n=TILES), in_=kf_sb[i][:])
-            nc.sync.dma_start(out=v_rows[rows, :].rearrange("(p n) f -> p (n f)", n=TILES), in_=v_sb[:])
+            kf = kf_rows[rows].rearrange("(p n) h f -> p n h f", n=TILES)
+            nc.sync.dma_start(out=kf[:, :, :, 0:NOPE], in_=nope_sb[:])
+            nc.sync.dma_start(
+                out=v_rows[rows, :].rearrange("(p n) f -> p (n f)", n=TILES),
+                in_=v_sb[:].rearrange("p n h f -> p (n h f)"),
+            )
 
         def run(stage, i):
             if 0 <= i < ROUNDS:
                 stage(i)
 
         for step in range(ROUNDS + 4):
-            run(norm_and_rotate, step - 2)
-            run(transpose_x, step)
+            run(normalise, step - 2)
             run(transpose_h, step - 3)
+            run(transpose_x, step)
+            run(quantise_h, step - 3)
+            run(quantise_x, step)
             run(down_project, step - 1)
+            run(rotate_and_store, step - 1)
             run(up_project_and_store, step - 4)

@@ -146,25 +146,25 @@ def tile_multiheadlatentattention_pb_t_kernel(tc, x, w_dkv, kv_a_norm, w_ukv, ou
         )
 
         x_grouped, x_codes, x_scales = {}, {}, {}
-        latent_ps, inv_rms, key_sb = {}, {}, {}
+        latent_ps, key_ps, sum_sq, inv_rms, key_sb = {}, {}, {}, {}, {}
         h_sb, h_grouped, h_codes, h_scales = {}, {}, {}, {}
 
-        def transpose_x(i):
+        def transpose_x(i, n):
             words = x_sb[i][:].bitcast(F32)
             n_words = D_MODEL // 2
-            x_grouped[i] = work.tile([P, TILES * n_words], F32, name="x_grouped", align_bytes=64)
-            for n in range(TILES):
-                xt_ps = psum_x.tile([P, 2 * X_PASSES, P], F32, name="xt_ps")
-                for a in range(2 * X_PASSES):
-                    first = n * n_words + a * P
-                    nc.tensor.transpose(xt_ps[:, a, :], words[:, first : first + P], identity[:])
-                copy = nc.scalar.copy if n == 0 else nc.vector.tensor_copy
-                copy(
-                    out=x_grouped[i][:, n * n_words : (n + 1) * n_words].rearrange(
-                        "p (g r u) -> p g r u", g=X_PASSES, u=2
-                    ),
-                    in_=xt_ps[:].rearrange("p (g u) r -> p g r u", u=2),
-                )
+            if n == 0:
+                x_grouped[i] = work.tile([P, TILES * n_words], F32, name="x_grouped", align_bytes=64)
+            xt_ps = psum_x.tile([P, 2 * X_PASSES, P], F32, name="xt_ps")
+            for a in range(2 * X_PASSES):
+                first = n * n_words + a * P
+                nc.tensor.transpose(xt_ps[:, a, :], words[:, first : first + P], identity[:])
+            copy = nc.scalar.copy if n == 0 else nc.vector.tensor_copy
+            copy(
+                out=x_grouped[i][:, n * n_words : (n + 1) * n_words].rearrange(
+                    "p (g r u) -> p g r u", g=X_PASSES, u=2
+                ),
+                in_=xt_ps[:].rearrange("p (g u) r -> p g r u", u=2),
+            )
 
         def quantise_x(i):
             x_codes[i] = work.tile([P, TILES * X_PASSES * P], U32, name="x_codes", align_bytes=64)
@@ -173,36 +173,38 @@ def tile_multiheadlatentattention_pb_t_kernel(tc, x, w_dkv, kv_a_norm, w_ukv, ou
                 out=x_codes[i][:].bitcast(FP8X4), scales=x_scales[i][:], in_=x_grouped[i][:].bitcast(BF16)
             )
 
-        def down_project(i):
-            key_ps = psum_one.tile([P, TILES, ROPE], F32, name="key_ps")
-            sum_sq = work.tile([P, TILES], F32, name="sum_sq")
-            for n in range(TILES):
-                latent_ps[i, n] = psum_c.tile([P, LATENT], F32, name="latent_ps")
-                for out, cols in (
-                    (latent_ps[i, n][:], slice(0, LATENT)),
-                    (key_ps[:, n, :], slice(LATENT, LATENT + ROPE)),
-                ):
-                    for g in range(X_PASSES):
-                        tokens = slice((n * X_PASSES + g) * P, (n * X_PASSES + g + 1) * P)
-                        nc.tensor.matmul_mx(
-                            out=out,
-                            lhsT=x_codes[i][:, tokens].bitcast(FP8X4),
-                            lhsT_scale=x_scales[i][:, tokens],
-                            rhs=wd_codes[:, g, cols].bitcast(FP8X4),
-                            rhs_scale=wd_scales[:, g, cols],
-                            start=(g == 0),
-                            stop=(g == X_PASSES - 1),
-                        )
-                squares = work.tile([P, LATENT], BF16, name="squares")
-                nc.scalar.activation(
-                    out=squares[:], in_=latent_ps[i, n][:], func=ACT.Square, accum_out=sum_sq[:, n : n + 1]
-                )
+        def down_project(i, n):
+            if n == 0:
+                key_ps[i] = psum_one.tile([P, TILES, ROPE], F32, name="key_ps")
+                sum_sq[i] = work.tile([P, TILES], F32, name="sum_sq")
+            latent_ps[i, n] = psum_c.tile([P, LATENT], F32, name="latent_ps")
+            for out, cols in (
+                (latent_ps[i, n][:], slice(0, LATENT)),
+                (key_ps[i][:, n, :], slice(LATENT, LATENT + ROPE)),
+            ):
+                for g in range(X_PASSES):
+                    tokens = slice((n * X_PASSES + g) * P, (n * X_PASSES + g + 1) * P)
+                    nc.tensor.matmul_mx(
+                        out=out,
+                        lhsT=x_codes[i][:, tokens].bitcast(FP8X4),
+                        lhsT_scale=x_scales[i][:, tokens],
+                        rhs=wd_codes[:, g, cols].bitcast(FP8X4),
+                        rhs_scale=wd_scales[:, g, cols],
+                        start=(g == 0),
+                        stop=(g == X_PASSES - 1),
+                    )
+            squares = work.tile([P, LATENT], BF16, name="squares")
+            nc.scalar.activation(
+                out=squares[:], in_=latent_ps[i, n][:], func=ACT.Square, accum_out=sum_sq[i][:, n : n + 1]
+            )
+
+        def finish_down_project(i):
             inv_rms[i] = work.tile([P, TILES], F32, name="inv_rms")
             nc.scalar.activation(
-                out=inv_rms[i][:], in_=sum_sq[:], func=ACT.Abs_reciprocal_sqrt, bias=eps[:], scale=1.0 / LATENT
+                out=inv_rms[i][:], in_=sum_sq[i][:], func=ACT.Abs_reciprocal_sqrt, bias=eps[:], scale=1.0 / LATENT
             )
             key_sb[i] = work.tile([P, TILES, 2, HALF], F32, name="key_sb")
-            nc.scalar.copy(out=key_sb[i][:].rearrange("p n a f -> p n (a f)"), in_=key_ps[:])
+            nc.scalar.copy(out=key_sb[i][:].rearrange("p n a f -> p n (a f)"), in_=key_ps[i][:])
 
         def rotate_and_store(i):
             first = (i % SEQ_ROUNDS) * TILES
@@ -293,16 +295,18 @@ def tile_multiheadlatentattention_pb_t_kernel(tc, x, w_dkv, kv_a_norm, w_ukv, ou
                 in_=v_sb[:].rearrange("p n h f -> p (n h f)"),
             )
 
-        def run(stage, i):
+        def run(stage, i, *tile):
             if 0 <= i < ROUNDS:
-                stage(i)
+                stage(i, *tile)
 
         for step in range(ROUNDS + 4):
             run(normalise, step - 2)
             run(transpose_h, step - 3)
-            run(transpose_x, step)
+            for n in range(TILES):
+                run(transpose_x, step, n)
+                run(down_project, step - 1, n)
             run(quantise_h, step - 3)
             run(quantise_x, step)
-            run(down_project, step - 1)
+            run(finish_down_project, step - 1)
             run(rotate_and_store, step - 1)
             run(up_project_and_store, step - 4)

@@ -129,7 +129,10 @@ def tile_multiheadlatentattention_pb_t_kernel(tc, x, w_dkv, kv_a_norm, w_ukv, ou
         wd_codes = keep.tile([P, X_PASSES, LATENT + ROPE], U32, align_bytes=64)
         wd_scales = keep.tile([P, X_PASSES, LATENT + ROPE], U8, align_bytes=64)
         for g in range(X_PASSES):
-            nc.vector.tensor_copy(out=wd_grouped[:, g], in_=wd_raw[:, g].rearrange("p t c -> p c t"))
+            nc.vector.tensor_copy(
+                out=wd_grouped[:, g].rearrange("p (c i) t -> p c t i", i=4),
+                in_=wd_raw[:, g].rearrange("p t (c i) -> p c t i", i=4),
+            )
         for g in range(X_PASSES):
             for cols in (slice(0, LATENT), slice(LATENT, LATENT + ROPE)):
                 nc.vector.quantize_mx(
@@ -146,25 +149,25 @@ def tile_multiheadlatentattention_pb_t_kernel(tc, x, w_dkv, kv_a_norm, w_ukv, ou
         )
 
         x_grouped, x_codes, x_scales = {}, {}, {}
-        latent_ps, key_ps, sum_sq, inv_rms, key_sb = {}, {}, {}, {}, {}
+        latent_ps, key_ps, inv_rms = {}, {}, {}
         h_sb, h_grouped, h_codes, h_scales = {}, {}, {}, {}
 
-        def transpose_x(i, n):
+        def transpose_x(i):
             words = x_sb[i][:].bitcast(F32)
             n_words = D_MODEL // 2
-            if n == 0:
-                x_grouped[i] = work.tile([P, TILES * n_words], F32, name="x_grouped", align_bytes=64)
-            xt_ps = psum_x.tile([P, 2 * X_PASSES, P], F32, name="xt_ps")
-            for a in range(2 * X_PASSES):
-                first = n * n_words + a * P
-                nc.tensor.transpose(xt_ps[:, a, :], words[:, first : first + P], identity[:])
-            copy = nc.scalar.copy if n == 0 else nc.vector.tensor_copy
-            copy(
-                out=x_grouped[i][:, n * n_words : (n + 1) * n_words].rearrange(
-                    "p (g r u) -> p g r u", g=X_PASSES, u=2
-                ),
-                in_=xt_ps[:].rearrange("p (g u) r -> p g r u", u=2),
-            )
+            x_grouped[i] = work.tile([P, TILES * n_words], F32, name="x_grouped", align_bytes=64)
+            for n in range(TILES):
+                xt_ps = psum_x.tile([P, 2 * X_PASSES, P], F32, name="xt_ps")
+                for a in range(2 * X_PASSES):
+                    first = n * n_words + a * P
+                    nc.tensor.transpose(xt_ps[:, a, :], words[:, first : first + P], identity[:])
+                copy = nc.scalar.copy if n == 0 else nc.vector.tensor_copy
+                copy(
+                    out=x_grouped[i][:, n * n_words : (n + 1) * n_words].rearrange(
+                        "p (g r u) -> p g r u", g=X_PASSES, u=2
+                    ),
+                    in_=xt_ps[:].rearrange("p (g u) r -> p g r u", u=2),
+                )
 
         def quantise_x(i):
             x_codes[i] = work.tile([P, TILES * X_PASSES * P], U32, name="x_codes", align_bytes=64)
@@ -173,53 +176,51 @@ def tile_multiheadlatentattention_pb_t_kernel(tc, x, w_dkv, kv_a_norm, w_ukv, ou
                 out=x_codes[i][:].bitcast(FP8X4), scales=x_scales[i][:], in_=x_grouped[i][:].bitcast(BF16)
             )
 
-        def down_project(i, n):
-            if n == 0:
-                key_ps[i] = psum_one.tile([P, TILES, ROPE], F32, name="key_ps")
-                sum_sq[i] = work.tile([P, TILES], F32, name="sum_sq")
-            latent_ps[i, n] = psum_c.tile([P, LATENT], F32, name="latent_ps")
-            for out, cols in (
-                (latent_ps[i, n][:], slice(0, LATENT)),
-                (key_ps[i][:, n, :], slice(LATENT, LATENT + ROPE)),
-            ):
-                for g in range(X_PASSES):
-                    tokens = slice((n * X_PASSES + g) * P, (n * X_PASSES + g + 1) * P)
-                    nc.tensor.matmul_mx(
-                        out=out,
-                        lhsT=x_codes[i][:, tokens].bitcast(FP8X4),
-                        lhsT_scale=x_scales[i][:, tokens],
-                        rhs=wd_codes[:, g, cols].bitcast(FP8X4),
-                        rhs_scale=wd_scales[:, g, cols],
-                        start=(g == 0),
-                        stop=(g == X_PASSES - 1),
-                    )
-            squares = work.tile([P, LATENT], BF16, name="squares")
-            nc.scalar.activation(
-                out=squares[:], in_=latent_ps[i, n][:], func=ACT.Square, accum_out=sum_sq[i][:, n : n + 1]
-            )
-
-        def finish_down_project(i):
+        def down_project(i):
+            key_ps[i] = psum_one.tile([P, TILES, ROPE], F32, name="key_ps")
+            sum_sq = work.tile([P, TILES], F32, name="sum_sq")
+            for n in range(TILES):
+                latent_ps[i, n] = psum_c.tile([P, LATENT], F32, name="latent_ps")
+                for out, cols in (
+                    (latent_ps[i, n][:], slice(0, LATENT)),
+                    (key_ps[i][:, n, :], slice(LATENT, LATENT + ROPE)),
+                ):
+                    for g in range(X_PASSES):
+                        tokens = slice((n * X_PASSES + g) * P, (n * X_PASSES + g + 1) * P)
+                        nc.tensor.matmul_mx(
+                            out=out,
+                            lhsT=x_codes[i][:, tokens].bitcast(FP8X4),
+                            lhsT_scale=x_scales[i][:, tokens],
+                            rhs=wd_codes[:, g, cols].bitcast(FP8X4),
+                            rhs_scale=wd_scales[:, g, cols],
+                            start=(g == 0),
+                            stop=(g == X_PASSES - 1),
+                        )
+                squares = work.tile([P, LATENT], BF16, name="squares")
+                nc.scalar.activation(
+                    out=squares[:], in_=latent_ps[i, n][:], func=ACT.Square, accum_out=sum_sq[:, n : n + 1]
+                )
             inv_rms[i] = work.tile([P, TILES], F32, name="inv_rms")
             nc.scalar.activation(
-                out=inv_rms[i][:], in_=sum_sq[i][:], func=ACT.Abs_reciprocal_sqrt, bias=eps[:], scale=1.0 / LATENT
+                out=inv_rms[i][:], in_=sum_sq[:], func=ACT.Abs_reciprocal_sqrt, bias=eps[:], scale=1.0 / LATENT
             )
-            key_sb[i] = work.tile([P, TILES, 2, HALF], F32, name="key_sb")
-            nc.scalar.copy(out=key_sb[i][:].rearrange("p n a f -> p n (a f)"), in_=key_ps[i][:])
 
         def rotate_and_store(i):
             first = (i % SEQ_ROUNDS) * TILES
             halves = [P, TILES, 2, HALF]
+            key_sb = work.tile(halves, F32, name="key_sb")
+            nc.vector.tensor_copy(out=key_sb[:].rearrange("p n a f -> p n (a f)"), in_=key_ps[i][:])
             key_cos = work.tile(halves, F32, name="key_cos")
             nc.gpsimd.tensor_tensor(
                 out=key_cos[:],
-                in0=key_sb[i][:],
+                in0=key_sb[:],
                 in1=cos_t[:, first : first + TILES, :].unsqueeze(2).to_broadcast(halves),
                 op=ALU.mult,
             )
             key_sin = work.tile(halves, F32, name="key_sin")
             nc.gpsimd.tensor_tensor(
                 out=key_sin[:],
-                in0=key_sb[i][:],
+                in0=key_sb[:],
                 in1=sin_t[:, first : first + TILES, :].unsqueeze(2).to_broadcast(halves),
                 op=ALU.mult,
             )
@@ -257,7 +258,7 @@ def tile_multiheadlatentattention_pb_t_kernel(tc, x, w_dkv, kv_a_norm, w_ukv, ou
                     first = n * n_words + u * P
                     nc.tensor.transpose(ht_ps[:, n, u, :], words[:, first : first + P], identity[:])
             h_grouped[i] = work.tile([P, TILES * n_words], F32, name="h_grouped", align_bytes=64)
-            nc.vector.tensor_copy(
+            nc.scalar.copy(
                 out=h_grouped[i][:].rearrange("p (n r u) -> p n r u", n=TILES, u=2),
                 in_=ht_ps[:].rearrange("p n u r -> p n r u"),
             )
@@ -295,18 +296,16 @@ def tile_multiheadlatentattention_pb_t_kernel(tc, x, w_dkv, kv_a_norm, w_ukv, ou
                 in_=v_sb[:].rearrange("p n h f -> p (n h f)"),
             )
 
-        def run(stage, i, *tile):
+        def run(stage, i):
             if 0 <= i < ROUNDS:
-                stage(i, *tile)
+                stage(i)
 
         for step in range(ROUNDS + 4):
+            run(rotate_and_store, step - 2)
             run(normalise, step - 2)
             run(transpose_h, step - 3)
-            for n in range(TILES):
-                run(transpose_x, step, n)
-                run(down_project, step - 1, n)
+            run(transpose_x, step)
             run(quantise_h, step - 3)
             run(quantise_x, step)
-            run(finish_down_project, step - 1)
-            run(rotate_and_store, step - 1)
+            run(down_project, step - 1)
             run(up_project_and_store, step - 4)

import math
from contextlib import ExitStack

import concourse.mybir as mybir
from concourse.masks import make_identity

F32 = mybir.dt.float32
BF16 = mybir.dt.bfloat16
I32 = mybir.dt.int32
U32 = mybir.dt.uint32
U8 = mybir.dt.uint8
FP8X4 = mybir.dt.float8_e4m3fn_x4
ALU = mybir.AluOpType
ACT = mybir.ActivationFunctionType

P = 128
PACK = 4
K_PASS = P * PACK

TOKENS = 2 * 2048
SEQ = 2048
D_MODEL = 1024
LATENT = 512
ROPE = 128
HALF = ROPE // 2
HEADS = 2
NOPE = 64
V_DIM = 64
KV_OUT = HEADS * (NOPE + V_DIM)
EPS = 1e-6
THETA = 10000.0

X_PASSES = D_MODEL // K_PASS
TILES = 2
ROUND = TILES * P
ROUNDS = TOKENS // ROUND
SEQ_ROUNDS = SEQ // ROUND

ROUND_MAGIC = 12582912.0

FLOPS = 2 * TOKENS * D_MODEL * (LATENT + ROPE) + 2 * TOKENS * LATENT * KV_OUT


def tile_multiheadlatentattention_pb_t_kernel(tc, x, w_dkv, kv_a_norm, w_ukv, out_0, out_1):
    nc = tc.nc
    x_rows = x.flatten_outer_dims()
    kf_rows = out_0.rearrange("b s h f -> (b s) h f")
    v_rows = out_1.rearrange("b s h f -> (b s) (h f)")

    with ExitStack() as ctx:
        keep = ctx.enter_context(tc.tile_pool(name="keep", bufs=1))
        x_pool = ctx.enter_context(tc.tile_pool(name="x_pool", bufs=ROUNDS))
        work = ctx.enter_context(tc.tile_pool(name="work", bufs=4))
        psum_x = ctx.enter_context(tc.psum_pool(name="psum_x", bufs=2))
        psum_c = ctx.enter_context(tc.psum_pool(name="psum_c", bufs=3))
        psum_one = ctx.enter_context(tc.psum_pool(name="psum_one", bufs=1))
        ctx.enter_context(tc.manual_schedule())

        wd_raw = keep.tile([P, X_PASSES, PACK, LATENT + ROPE], BF16)
        for g in range(X_PASSES):
            nc.sync.dma_start(
                out=wd_raw[:, g].rearrange("p (u e) c -> p u (e c)", u=2),
                in_=w_dkv[g * K_PASS : (g + 1) * K_PASS, :].rearrange("(u p e) c -> p u (e c)", u=2, e=2),
            )
        x_sb = {}
        for i in range(ROUNDS):
            x_sb[i] = x_pool.tile([P, TILES * D_MODEL], BF16, name="x_sb")
            nc.sync.dma_start(
                out=x_sb[i][:],
                in_=x_rows[i * ROUND : (i + 1) * ROUND, :].rearrange("(p n) d -> p (n d)", n=TILES),
            )
        wu_raw = keep.tile([P, PACK, KV_OUT], BF16)
        nc.scalar.dma_start(
            out=wu_raw[:].rearrange("p (u e) n -> p u (e n)", u=2),
            in_=w_ukv.rearrange("(u p e) n -> p u (e n)", u=2, e=2),
        )
        gain = keep.tile([P, LATENT], BF16)
        nc.scalar.dma_start(out=gain[:], in_=kv_a_norm.partition_broadcast(P))

        n_pos = SEQ // P
        pos_int = keep.tile([P, n_pos], I32)
        nc.gpsimd.iota(pos_int[:], pattern=[[ROUND, SEQ_ROUNDS], [1, TILES]], base=0, channel_multiplier=TILES)
        identity = keep.tile([P, P], F32)
        make_identity(nc, identity[:])
        one = keep.tile([P, 1], F32)
        nc.vector.memset(one[:], 1.0)
        freq = keep.tile([P, HALF], F32)
        nc.vector.tensor_scalar_mul(out=freq[:, 0:1], in0=one[:], scalar1=1.0 / (2.0 * math.pi))
        filled = 1
        while filled < HALF:
            nc.vector.tensor_scalar_mul(
                out=freq[:, filled : 2 * filled], in0=freq[:, 0:filled], scalar1=THETA ** (-filled / HALF)
            )
            filled *= 2
        pos = keep.tile([P, n_pos], F32)
        nc.vector.tensor_copy(out=pos[:], in_=pos_int[:])
        table_shape = [P, n_pos, HALF]
        turns = keep.tile(table_shape, F32)
        nc.vector.tensor_tensor(
            out=turns[:],
            in0=pos[:].unsqueeze(2).to_broadcast(table_shape),
            in1=freq[:].unsqueeze(1).to_broadcast(table_shape),
            op=ALU.mult,
        )
        whole = keep.tile(table_shape, F32)
        nc.vector.tensor_scalar(
            out=whole[:], in0=turns[:], scalar1=ROUND_MAGIC, scalar2=ROUND_MAGIC, op0=ALU.add, op1=ALU.subtract
        )
        frac = keep.tile(table_shape, F32)
        nc.vector.tensor_tensor(out=frac[:], in0=turns[:], in1=whole[:], op=ALU.subtract)
        quarter_turn = keep.tile([P, 1], F32)
        nc.vector.tensor_scalar_mul(out=quarter_turn[:], in0=one[:], scalar1=math.pi / 2.0)
        eps = keep.tile([P, 1], F32)
        nc.vector.tensor_scalar_mul(out=eps[:], in0=one[:], scalar1=EPS)

        wu_grouped = keep.tile([P, KV_OUT, PACK], BF16, align_bytes=64)
        nc.scalar.copy(out=wu_grouped[:], in_=wu_raw[:].rearrange("p t n -> p n t"))

        sin_t = keep.tile(table_shape, F32)
        nc.scalar.activation(out=sin_t[:], in_=frac[:], func=ACT.Sin, scale=2.0 * math.pi)
        abs_frac = keep.tile(table_shape, F32)
        nc.scalar.activation(out=abs_frac[:], in_=frac[:], func=ACT.Abs)
        cos_t = keep.tile(table_shape, F32)
        nc.scalar.activation(
            out=cos_t[:], in_=abs_frac[:], func=ACT.Sin, bias=quarter_turn[:], scale=-2.0 * math.pi
        )

        wd_grouped = keep.tile([P, X_PASSES, LATENT + ROPE, PACK], BF16, align_bytes=64)
        wd_codes = keep.tile([P, X_PASSES, LATENT + ROPE], U32, align_bytes=64)
        wd_scales = keep.tile([P, X_PASSES, LATENT + ROPE], U8, align_bytes=64)
        for g in range(X_PASSES):
            nc.vector.tensor_copy(
                out=wd_grouped[:, g].rearrange("p (c i) t -> p c t i", i=4),
                in_=wd_raw[:, g].rearrange("p t (c i) -> p c t i", i=4),
            )
        for g in range(X_PASSES):
            for cols in (slice(0, LATENT), slice(LATENT, LATENT + ROPE)):
                nc.vector.quantize_mx(
                    out=wd_codes[:, g, cols].bitcast(FP8X4),
                    scales=wd_scales[:, g, cols],
                    in_=wd_grouped[:, g, cols, :].rearrange("p c t -> p (c t)"),
                )
        wu_codes = keep.tile([P, KV_OUT], U32, align_bytes=64)
        wu_scales = keep.tile([P, KV_OUT], U8, align_bytes=64)
        nc.vector.quantize_mx(
            out=wu_codes[:].bitcast(FP8X4),
            scales=wu_scales[:],
            in_=wu_grouped[:].rearrange("p n t -> p (n t)"),
        )

        x_grouped, x_codes, x_scales = {}, {}, {}
        latent_ps, key_ps, inv_rms = {}, {}, {}
        h_sb, h_grouped, h_codes, h_scales = {}, {}, {}, {}

        def transpose_x(i):
            words = x_sb[i][:].bitcast(F32)
            n_words = D_MODEL // 2
            x_grouped[i] = work.tile([P, TILES * n_words], F32, name="x_grouped", align_bytes=64)
            for n in range(TILES):
                xt_ps = psum_x.tile([P, 2 * X_PASSES, P], F32, name="xt_ps")
                for a in range(2 * X_PASSES):
                    first = n * n_words + a * P
                    nc.tensor.transpose(xt_ps[:, a, :], words[:, first : first + P], identity[:])
                copy = nc.scalar.copy if n == 0 else nc.vector.tensor_copy
                copy(
                    out=x_grouped[i][:, n * n_words : (n + 1) * n_words].rearrange(
                        "p (g r u) -> p g r u", g=X_PASSES, u=2
                    ),
                    in_=xt_ps[:].rearrange("p (g u) r -> p g r u", u=2),
                )

        def quantise_x(i):
            x_codes[i] = work.tile([P, TILES * X_PASSES * P], U32, name="x_codes", align_bytes=64)
            x_scales[i] = work.tile([P, TILES * X_PASSES * P], U8, name="x_scales", align_bytes=64)
            nc.vector.quantize_mx(
                out=x_codes[i][:].bitcast(FP8X4), scales=x_scales[i][:], in_=x_grouped[i][:].bitcast(BF16)
            )

        def down_project(i):
            key_ps[i] = psum_one.tile([P, TILES, ROPE], F32, name="key_ps")
            sum_sq = work.tile([P, TILES], F32, name="sum_sq")
            for n in range(TILES):
                latent_ps[i, n] = psum_c.tile([P, LATENT], F32, name="latent_ps")
                for out, cols in (
                    (latent_ps[i, n][:], slice(0, LATENT)),
                    (key_ps[i][:, n, :], slice(LATENT, LATENT + ROPE)),
                ):
                    for g in range(X_PASSES):
                        tokens = slice((n * X_PASSES + g) * P, (n * X_PASSES + g + 1) * P)
                        nc.tensor.matmul_mx(
                            out=out,
                            lhsT=x_codes[i][:, tokens].bitcast(FP8X4),
                            lhsT_scale=x_scales[i][:, tokens],
                            rhs=wd_codes[:, g, cols].bitcast(FP8X4),
                            rhs_scale=wd_scales[:, g, cols],
                            start=(g == 0),
                            stop=(g == X_PASSES - 1),
                        )
                squares = work.tile([P, LATENT], BF16, name="squares")
                nc.scalar.activation(
                    out=squares[:], in_=latent_ps[i, n][:], func=ACT.Square, accum_out=sum_sq[:, n : n + 1]
                )
            inv_rms[i] = work.tile([P, TILES], F32, name="inv_rms")
            nc.scalar.activation(
                out=inv_rms[i][:], in_=sum_sq[:], func=ACT.Abs_reciprocal_sqrt, bias=eps[:], scale=1.0 / LATENT
            )

        def rotate_and_store(i):
            first = (i % SEQ_ROUNDS) * TILES
            halves = [P, TILES, 2, HALF]
            key_sb = work.tile(halves, F32, name="key_sb")
            nc.vector.tensor_copy(out=key_sb[:].rearrange("p n a f -> p n (a f)"), in_=key_ps[i][:])
            key_cos = work.tile(halves, F32, name="key_cos")
            nc.gpsimd.tensor_tensor(
                out=key_cos[:],
                in0=key_sb[:],
                in1=cos_t[:, first : first + TILES, :].unsqueeze(2).to_broadcast(halves),
                op=ALU.mult,
            )
            key_sin = work.tile(halves, F32, name="key_sin")
            nc.gpsimd.tensor_tensor(
                out=key_sin[:],
                in0=key_sb[:],
                in1=sin_t[:, first : first + TILES, :].unsqueeze(2).to_broadcast(halves),
                op=ALU.mult,
            )
            rotated = work.tile(halves, F32, name="rotated")
            nc.gpsimd.tensor_tensor(
                out=rotated[:, :, 0, :], in0=key_cos[:, :, 0, :], in1=key_sin[:, :, 1, :], op=ALU.subtract
            )
            nc.gpsimd.tensor_tensor(
                out=rotated[:, :, 1, :], in0=key_cos[:, :, 1, :], in1=key_sin[:, :, 0, :], op=ALU.add
            )
            kf = kf_rows[i * ROUND : (i + 1) * ROUND].rearrange("(p n) h f -> p n h f", n=TILES)
            for head in range(HEADS):
                nc.sync.dma_start(
                    out=kf[:, :, head, NOPE : NOPE + ROPE], in_=rotated[:].rearrange("p n a f -> p n (a f)")
                )

        def normalise(i):
            h_sb[i] = work.tile([P, TILES * LATENT], BF16, name="h_sb")
            for n in range(TILES):
                nc.vector.scalar_tensor_tensor(
                    out=h_sb[i][:, n * LATENT : (n + 1) * LATENT],
                    in0=latent_ps[i, n][:],
                    scalar=inv_rms[i][:, n : n + 1],
                    in1=gain[:],
                    op0=ALU.mult,
                    op1=ALU.mult,
                )

        def transpose_h(i):
            words = h_sb[i][:].bitcast(F32)
            n_words = LATENT // 2
            ht_ps = psum_one.tile([P, TILES, 2, P], F32, name="ht_ps")
            for n in range(TILES):
                for u in range(2):
                    first = n * n_words + u * P
                    nc.tensor.transpose(ht_ps[:, n, u, :], words[:, first : first + P], identity[:])
            h_grouped[i] = work.tile([P, TILES * n_words], F32, name="h_grouped", align_bytes=64)
            nc.scalar.copy(
                out=h_grouped[i][:].rearrange("p (n r u) -> p n r u", n=TILES, u=2),
                in_=ht_ps[:].rearrange("p n u r -> p n r u"),
            )

        def quantise_h(i):
            h_codes[i] = work.tile([P, TILES * P], U32, name="h_codes", align_bytes=64)
            h_scales[i] = work.tile([P, TILES * P], U8, name="h_scales", align_bytes=64)
            nc.vector.quantize_mx(
                out=h_codes[i][:].bitcast(FP8X4), scales=h_scales[i][:], in_=h_grouped[i][:].bitcast(BF16)
            )

        def up_project_and_store(i):
            kv_ps = psum_one.tile([P, TILES, KV_OUT], F32, name="kv_ps")
            for n in range(TILES):
                tokens = slice(n * P, (n + 1) * P)
                nc.tensor.matmul_mx(
                    out=kv_ps[:, n, :],
                    lhsT=h_codes[i][:, tokens].bitcast(FP8X4),
                    lhsT_scale=h_scales[i][:, tokens],
                    rhs=wu_codes[:].bitcast(FP8X4),
                    rhs_scale=wu_scales[:],
                    start=True,
                    stop=True,
                )
            kv = kv_ps[:].rearrange("p n (h f) -> p n h f", h=HEADS)
            nope_sb = work.tile([P, TILES, HEADS, NOPE], F32, name="nope_sb")
            nc.scalar.copy(out=nope_sb[:], in_=kv[:, :, :, 0:NOPE])
            v_sb = work.tile([P, TILES, HEADS, V_DIM], F32, name="v_sb")
            nc.scalar.copy(out=v_sb[:], in_=kv[:, :, :, NOPE : NOPE + V_DIM])
            rows = slice(i * ROUND, (i + 1) * ROUND)
            kf = kf_rows[rows].rearrange("(p n) h f -> p n h f", n=TILES)
            nc.sync.dma_start(out=kf[:, :, :, 0:NOPE], in_=nope_sb[:])
            nc.sync.dma_start(
                out=v_rows[rows, :].rearrange("(p n) f -> p (n f)", n=TILES),
                in_=v_sb[:].rearrange("p n h f -> p (n h f)"),
            )

        def run(stage, i):
            if 0 <= i < ROUNDS:
                stage(i)

        for step in range(ROUNDS + 4):
            run(rotate_and_store, step - 2)
            run(normalise, step - 2)
            run(transpose_h, step - 3)
            run(transpose_x, step)
            run(quantise_h, step - 3)
            run(quantise_x, step)
            run(down_project, step - 1)
            run(up_project_and_store, step - 4)
